import numpy as np
import ml_dtypes


def mxq(x, axis, fmt="e4m3"):
    dtype, down = {"e4m3": (ml_dtypes.float8_e4m3fn, 7), "e5m2": (ml_dtypes.float8_e5m2, 14)}[fmt]
    v = np.moveaxis(np.asarray(x, np.float32).astype(ml_dtypes.bfloat16).astype(np.float64), axis, -1)
    blocks = v.reshape(v.shape[:-1] + (-1, 32))
    amax = np.abs(blocks).max(-1, keepdims=True)
    byte = np.maximum(np.where(amax > 0, np.frexp(amax)[1] - 1 + 127, 0) - down, 1)
    scale = np.exp2(byte - 127.0)
    codes = (blocks / scale).astype(np.float32).astype(dtype).astype(np.float64)
    return np.moveaxis((codes * scale).reshape(v.shape), -1, axis)


WIDE = False


def mx_kscale(k):
    if not WIDE:
        return np.ones(k)
    levels = np.array([10, -10, 5, -5, 0])
    a = np.random.permutation(np.resize(levels, k // 512 * 4)).reshape(k // 512, 4)
    idx = np.arange(k)
    return np.exp2(a[idx // 512, idx % 128 // 32])


BF16 = ml_dtypes.bfloat16


def bf(x):
    return np.asarray(x, np.float32).astype(BF16)


def f64(x):
    return np.asarray(x).astype(np.float64)


B, C, HI, WI, KH, KW, SH, SW, F1, F2, F3 = 2, 16, 22, 22, 8, 8, 2, 2, 1024, 128, 64
K1 = C * KH * KW
HO = (HI - KH) // SH + 1
WO = (WI - KW) // SW + 1
L = HO * WO


def unfold(x):
    cols = [x[:, :, i:i + (HO - 1) * SH + 1:SH, j:j + (WO - 1) * SW + 1:SW] for i in range(KH) for j in range(KW)]
    return np.stack(cols, axis=2).reshape(B, K1, L)


def setup_inputs():
    sc = mx_kscale(K1)[::KH * KW]
    s = np.repeat(sc, KH * KW)
    t = mx_kscale(F1)
    return {"x": bf(np.random.standard_normal((B, C, HI, WI)) * sc[None, :, None, None]),
            "w1": bf(np.random.standard_normal((K1, F1)) / np.sqrt(K1) / s[:, None] * t),
            "b1": bf(np.random.standard_normal(F1) * 0.3 * t),
            "w2": bf(np.random.standard_normal((F1, F2)) * 1.4 / np.sqrt(F1) / t[:, None]),
            "b2": bf(np.random.standard_normal(F2) * 0.3)}


def reference(x, w1, b1, w2, b2):
    p = unfold(f64(x)).transpose(0, 2, 1)
    h1 = np.maximum((mxq(p, 2, "e4m3") @ mxq(f64(w1), 0, "e4m3")) + f64(b1), 0.0)
    return np.maximum((mxq(h1, 2, "e4m3") @ mxq(f64(w2), 0, "e4m3")) + f64(b2), 0.0)

@@ -1,0 +1,154 @@
+import concourse.mybir as mybir
+
+BF16 = mybir.dt.bfloat16
+F32 = mybir.dt.float32
+U32 = mybir.dt.uint32
+U8 = mybir.dt.uint8
+FP8X4 = mybir.dt.float8_e4m3fn_x4
+
+P = 128
+PACK = 4
+PASSES = 2
+
+IMAGES, CHANNELS, HEIGHT, WIDTH = 2, 16, 22, 22
+WINDOW, STRIDE, GRID = 8, 2, 8
+TOKENS = IMAGES * GRID * GRID
+F1 = 1024
+F2 = 128
+F_TILE = 128
+F_HALF = 512
+ROWS_KEPT = STRIDE * (GRID - 1) + 1
+RUN = ROWS_KEPT * WIDTH
+U_STEP = STRIDE * WIDTH
+VECTOR_COLS = 256
+
+FLOPS = 2 * TOKENS * 1024 * F1 + 2 * TOKENS * F1 * F2
+
+
+def regroup(copy, grouped, raw):
+    copy(
+        out=grouped.rearrange("p (c i) t -> p c t i", i=4),
+        in_=raw.rearrange("p t (c i) -> p c t i", i=4),
+    )
+
+
+def tile_mlpconv2d_pa_s_kernel(tc, x, w1, b1, w2, b2, out):
+    nc = tc.nc
+    with tc.tile_pool(name="keep", bufs=1) as keep, tc.tile_pool(name="stream", bufs=4) as stream, tc.psum_pool(
+        name="psum", bufs=1
+    ) as psum:
+        rows = keep.tile([P, IMAGES, GRID * U_STEP], BF16)
+        for i in range(WINDOW):
+            queue = nc.scalar if i < 6 else nc.gpsimd
+            queue.dma_start(
+                out=rows[i:P:WINDOW, :, 0:RUN],
+                in_=x[:, :, i : i + ROWS_KEPT, :].rearrange("n c h w -> c n (h w)"),
+            )
+        w1_view = w1.rearrange("(p g t) f -> p g t f", g=PASSES, t=PACK)
+        w1_raw = {}
+        for half in range(2):
+            for g in range(PASSES):
+                raw = stream.tile([P, PACK, F_HALF], BF16, name="w1_raw")
+                nc.sync.dma_start(out=raw[:], in_=w1_view[:, g, :, half * F_HALF : (half + 1) * F_HALF])
+                w1_raw[(half, g)] = raw
+        b1_cols = keep.tile([P, F1 // P], BF16)
+        with nc.allow_non_contiguous_dma(reason="1,024 bias values, one to a partition"):
+            nc.gpsimd.dma_start(out=b1_cols[:], in_=b1.rearrange("(m p) -> p m", p=P))
+        w2_raw = keep.tile([P, PASSES * PACK, F2], BF16)
+        nc.gpsimd.dma_start(out=w2_raw[:], in_=w2.rearrange("(g t p) n -> p (g t) n", t=PACK, p=P))
+        b2_all = keep.tile([P, F2], BF16)
+        nc.gpsimd.dma_start(out=b2_all[:], in_=b2.partition_broadcast(P))
+
+        p_grouped = keep.tile([P, PASSES, TOKENS, PACK], BF16, align_bytes=64)
+        p_codes = keep.tile([P, PASSES, TOKENS], U32, align_bytes=64)
+        p_scales = keep.tile([P, PASSES, TOKENS], U8, align_bytes=64)
+        by_grid_row = rows[:].rearrange("p n (u r) -> p (n u) r", r=U_STEP)
+        for g in range(PASSES):
+            copy = nc.vector.tensor_copy if g == 0 else nc.scalar.copy
+            pairs = p_grouped[:, g].rearrange("p (a v) (h e) -> p h a v e", v=GRID, e=2)
+            for h in range(2):
+                first = PACK * g + 2 * h
+                copy(
+                    out=pairs[:, h],
+                    in_=by_grid_row[:, :, first : first + 2 * GRID].rearrange("p a (v e) -> p a v e", e=2),
+                )
+        nc.vector.quantize_mx(
+            out=p_codes[:].rearrange("p g r -> p (g r)").bitcast(FP8X4),
+            scales=p_scales[:].rearrange("p g r -> p (g r)"),
+            in_=p_grouped[:].rearrange("p g r t -> p (g r t)"),
+        )
+
+        w2_grouped = keep.tile([P, PASSES, F2, PACK], BF16, align_bytes=64)
+        w2_codes = keep.tile([P, PASSES, F2], U32, align_bytes=64)
+        w2_scales = keep.tile([P, PASSES, F2], U8, align_bytes=64)
+
+        w1_codes = keep.tile([P, PASSES, F1], U32, align_bytes=64)
+        w1_scales = keep.tile([P, PASSES, F1], U8, align_bytes=64)
+        h_codes = keep.tile([P, PASSES, TOKENS], U32, align_bytes=64)
+        h_scales = keep.tile([P, PASSES, TOKENS], U8, align_bytes=64)
+        out_acc = psum.tile([P, F2], F32)
+
+        for half in range(2):
+            for g in range(PASSES):
+                raw = w1_raw[(half, g)]
+                grouped = stream.tile([P, F_HALF, PACK], BF16, align_bytes=64, name="w1_grouped")
+                regroup(nc.vector.tensor_copy, grouped[:, 0:VECTOR_COLS, :], raw[:, :, 0:VECTOR_COLS])
+                regroup(nc.scalar.copy, grouped[:, VECTOR_COLS:F_HALF, :], raw[:, :, VECTOR_COLS:F_HALF])
+                for lo, hi in ((0, VECTOR_COLS), (VECTOR_COLS, F_HALF)):
+                    cols = slice(half * F_HALF + lo, half * F_HALF + hi)
+                    nc.vector.quantize_mx(
+                        out=w1_codes[:, g, cols].bitcast(FP8X4),
+                        scales=w1_scales[:, g, cols],
+                        in_=grouped[:, lo:hi, :].rearrange("p f t -> p (f t)"),
+                    )
+            if half == 0:
+                for g in range(PASSES):
+                    regroup(nc.scalar.copy, w2_grouped[:, g], w2_raw[:, PACK * g : PACK * (g + 1), :])
+                nc.vector.quantize_mx(
+                    out=w2_codes[:].rearrange("p g n -> p (g n)").bitcast(FP8X4),
+                    scales=w2_scales[:].rearrange("p g n -> p (g n)"),
+                    in_=w2_grouped[:].rearrange("p g n t -> p (g n t)"),
+                )
+
+            h_acc = psum.tile([P, PACK, TOKENS], F32, name="h_acc%d" % half)
+            for t in range(PACK):
+                cols = slice(half * F_HALF + t * F_TILE, half * F_HALF + (t + 1) * F_TILE)
+                for g in range(PASSES):
+                    nc.tensor.matmul_mx(
+                        out=h_acc[:, t, :],
+                        lhsT=w1_codes[:, g, cols].bitcast(FP8X4),
+                        lhsT_scale=w1_scales[:, g, cols],
+                        rhs=p_codes[:, g, :].bitcast(FP8X4),
+                        rhs_scale=p_scales[:, g, :],
+                        start=(g == 0),
+                        stop=(g == PASSES - 1),
+                    )
+            h_biased = stream.tile([P, TOKENS, PACK], BF16, name="h_biased")
+            nc.vector.tensor_tensor(
+                out=h_biased[:],
+                in0=h_acc[:].rearrange("p t r -> p r t"),
+                in1=b1_cols[:, PACK * half : PACK * (half + 1)].unsqueeze(1).to_broadcast([P, TOKENS, PACK]),
+                op=mybir.AluOpType.add,
+            )
+            h_grouped = stream.tile([P, TOKENS, PACK], BF16, align_bytes=64, name="h_grouped")
+            nc.vector.tensor_scalar_max(out=h_grouped[:], in0=h_biased[:], scalar1=0.0)
+            nc.vector.quantize_mx(
+                out=h_codes[:, half, :].bitcast(FP8X4),
+                scales=h_scales[:, half, :],
+                in_=h_grouped[:].rearrange("p r t -> p (r t)"),
+            )
+            nc.tensor.matmul_mx(
+                out=out_acc[:],
+                lhsT=h_codes[:, half, :].bitcast(FP8X4),
+                lhsT_scale=h_scales[:, half, :],
+                rhs=w2_codes[:, half, :].bitcast(FP8X4),
+                rhs_scale=w2_scales[:, half, :],
+                start=(half == 0),
+                stop=(half == 1),
+            )
+
+        biased = keep.tile([P, F2], F32)
+        nc.vector.tensor_tensor(out=biased[:], in0=out_acc[:], in1=b2_all[:], op=mybir.AluOpType.add)
+        result = keep.tile([P, F2], F32)
+        nc.vector.tensor_scalar_max(out=result[:], in0=biased[:], scalar1=0.0)
+        nc.sync.dma_start(out=out.flatten_outer_dims(), in_=result[:])

@@ -1,10 +1,12 @@
 import concourse.mybir as mybir
+from concourse.masks import make_identity
 
 BF16 = mybir.dt.bfloat16
 F32 = mybir.dt.float32
 U32 = mybir.dt.uint32
 U8 = mybir.dt.uint8
 FP8X4 = mybir.dt.float8_e4m3fn_x4
+ADD = mybir.AluOpType.add
 
 P = 128
 PACK = 4
@@ -16,10 +18,13 @@ TOKENS = IMAGES * GRID * GRID
 F1 = 1024
 F2 = 128
 F_TILE = 128
-F_HALF = 512
+F_HALF = PACK * F_TILE
+HALVES = F1 // F_HALF
 ROWS_KEPT = STRIDE * (GRID - 1) + 1
 RUN = ROWS_KEPT * WIDTH
 U_STEP = STRIDE * WIDTH
+B1_ROWS = F1 // P
+QUANT_COLS = 256
 VECTOR_COLS = 256
 
 FLOPS = 2 * TOKENS * 1024 * F1 + 2 * TOKENS * F1 * F2
@@ -34,9 +39,11 @@ def regroup(copy, grouped, raw):
 
 def tile_mlpconv2d_pa_s_kernel(tc, x, w1, b1, w2, b2, out):
     nc = tc.nc
-    with tc.tile_pool(name="keep", bufs=1) as keep, tc.tile_pool(name="stream", bufs=4) as stream, tc.psum_pool(
-        name="psum", bufs=1
-    ) as psum:
+    with tc.tile_pool(name="keep", bufs=1) as keep, tc.psum_pool(name="psum", bufs=1) as psum:
+
+        def quantise(codes, scales, grouped):
+            nc.vector.quantize_mx(out=codes.bitcast(FP8X4), scales=scales, in_=grouped)
+
         rows = keep.tile([P, IMAGES, GRID * U_STEP], BF16)
         for i in range(WINDOW):
             queue = nc.scalar if i < 6 else nc.gpsimd
@@ -44,20 +51,18 @@ def tile_mlpconv2d_pa_s_kernel(tc, x, w1, b1, w2, b2, out):
                 out=rows[i:P:WINDOW, :, 0:RUN],
                 in_=x[:, :, i : i + ROWS_KEPT, :].rearrange("n c h w -> c n (h w)"),
             )
+        bias_rows = keep.tile([P, P], BF16)
+        nc.vector.memset(bias_rows[:], 0.0)
         w1_view = w1.rearrange("(p g t) f -> p g t f", g=PASSES, t=PACK)
-        w1_raw = {}
-        for half in range(2):
+        w1_raw = keep.tile([P, HALVES, PASSES, PACK, F_HALF], BF16)
+        for half in range(HALVES):
             for g in range(PASSES):
-                raw = stream.tile([P, PACK, F_HALF], BF16, name="w1_raw")
-                nc.sync.dma_start(out=raw[:], in_=w1_view[:, g, :, half * F_HALF : (half + 1) * F_HALF])
-                w1_raw[(half, g)] = raw
-        b1_cols = keep.tile([P, F1 // P], BF16)
-        with nc.allow_non_contiguous_dma(reason="1,024 bias values, one to a partition"):
-            nc.gpsimd.dma_start(out=b1_cols[:], in_=b1.rearrange("(m p) -> p m", p=P))
-        w2_raw = keep.tile([P, PASSES * PACK, F2], BF16)
-        nc.gpsimd.dma_start(out=w2_raw[:], in_=w2.rearrange("(g t p) n -> p (g t) n", t=PACK, p=P))
-        b2_all = keep.tile([P, F2], BF16)
-        nc.gpsimd.dma_start(out=b2_all[:], in_=b2.partition_broadcast(P))
+                nc.sync.dma_start(out=w1_raw[:, half, g], in_=w1_view[:, g, :, half * F_HALF : (half + 1) * F_HALF])
+            if half == 0:
+                nc.sync.dma_start(out=bias_rows[0:B1_ROWS, :], in_=b1.rearrange("(m p) -> m p", p=P))
+                nc.sync.dma_start(out=bias_rows[B1_ROWS : B1_ROWS + 1, :], in_=b2.unsqueeze(0))
+        w2_raw = keep.tile([P, PASSES, PACK, F2], BF16)
+        nc.sync.dma_start(out=w2_raw[:], in_=w2.rearrange("(g t p) n -> p g t n", t=PACK, p=P))
 
         p_grouped = keep.tile([P, PASSES, TOKENS, PACK], BF16, align_bytes=64)
         p_codes = keep.tile([P, PASSES, TOKENS], U32, align_bytes=64)
@@ -72,50 +77,61 @@ def tile_mlpconv2d_pa_s_kernel(tc, x, w1, b1, w2, b2, out):
                     out=pairs[:, h],
                     in_=by_grid_row[:, :, first : first + 2 * GRID].rearrange("p a (v e) -> p a v e", e=2),
                 )
-        nc.vector.quantize_mx(
-            out=p_codes[:].rearrange("p g r -> p (g r)").bitcast(FP8X4),
-            scales=p_scales[:].rearrange("p g r -> p (g r)"),
-            in_=p_grouped[:].rearrange("p g r t -> p (g r t)"),
-        )
+        for g in range(PASSES):
+            quantise(p_codes[:, g, :], p_scales[:, g, :], p_grouped[:, g].rearrange("p r t -> p (r t)"))
 
+        w1_grouped = keep.tile([P, HALVES, PASSES, F_HALF, PACK], BF16, align_bytes=64)
+        w1_codes = keep.tile([P, PASSES, F1], U32, align_bytes=64)
+        w1_scales = keep.tile([P, PASSES, F1], U8, align_bytes=64)
+
+        def prepare_w1(half):
+            for g in range(PASSES):
+                raw = w1_raw[:, half, g]
+                grouped = w1_grouped[:, half, g]
+                regroup(nc.vector.tensor_copy, grouped[:, 0:VECTOR_COLS, :], raw[:, :, 0:VECTOR_COLS])
+                regroup(nc.scalar.copy, grouped[:, VECTOR_COLS:F_HALF, :], raw[:, :, VECTOR_COLS:F_HALF])
+                for lo in range(0, F_HALF, QUANT_COLS):
+                    cols = slice(half * F_HALF + lo, half * F_HALF + lo + QUANT_COLS)
+                    quantise(
+                        w1_codes[:, g, cols],
+                        w1_scales[:, g, cols],
+                        grouped[:, lo : lo + QUANT_COLS, :].rearrange("p f t -> p (f t)"),
+                    )
+
+        ident = keep.tile([P, P], BF16)
+        make_identity(nc, ident[:])
+        bias_turned = psum.tile([P, P], BF16)
+        bias_cols = keep.tile([P, B1_ROWS + 1], BF16)
+        b2_spread = psum.tile([P, F2], F32)
+        b2_all = keep.tile([P, F2], F32)
+
+        def turn_biases():
+            nc.tensor.transpose(out=bias_turned[:], in_=bias_rows[:], identity=ident[:])
+            nc.vector.tensor_copy(out=bias_cols[:], in_=bias_turned[:, 0 : B1_ROWS + 1])
+            nc.tensor.matmul(
+                out=b2_spread[:],
+                lhsT=bias_cols[:, B1_ROWS : B1_ROWS + 1].to_broadcast([P, P]),
+                rhs=ident[:],
+                start=True,
+                stop=True,
+            )
+
+        h_acc = [psum.tile([P, PACK, TOKENS], F32, name="h_acc%d" % half) for half in range(HALVES)]
+        h_biased = keep.tile([P, HALVES, TOKENS, PACK], BF16)
+        h_grouped = keep.tile([P, HALVES, TOKENS, PACK], BF16, align_bytes=64)
+        h_codes = keep.tile([P, HALVES, TOKENS], U32, align_bytes=64)
+        h_scales = keep.tile([P, HALVES, TOKENS], U8, align_bytes=64)
         w2_grouped = keep.tile([P, PASSES, F2, PACK], BF16, align_bytes=64)
         w2_codes = keep.tile([P, PASSES, F2], U32, align_bytes=64)
         w2_scales = keep.tile([P, PASSES, F2], U8, align_bytes=64)
-
-        w1_codes = keep.tile([P, PASSES, F1], U32, align_bytes=64)
-        w1_scales = keep.tile([P, PASSES, F1], U8, align_bytes=64)
-        h_codes = keep.tile([P, PASSES, TOKENS], U32, align_bytes=64)
-        h_scales = keep.tile([P, PASSES, TOKENS], U8, align_bytes=64)
         out_acc = psum.tile([P, F2], F32)
 
-        for half in range(2):
-            for g in range(PASSES):
-                raw = w1_raw[(half, g)]
-                grouped = stream.tile([P, F_HALF, PACK], BF16, align_bytes=64, name="w1_grouped")
-                regroup(nc.vector.tensor_copy, grouped[:, 0:VECTOR_COLS, :], raw[:, :, 0:VECTOR_COLS])
-                regroup(nc.scalar.copy, grouped[:, VECTOR_COLS:F_HALF, :], raw[:, :, VECTOR_COLS:F_HALF])
-                for lo, hi in ((0, VECTOR_COLS), (VECTOR_COLS, F_HALF)):
-                    cols = slice(half * F_HALF + lo, half * F_HALF + hi)
-                    nc.vector.quantize_mx(
-                        out=w1_codes[:, g, cols].bitcast(FP8X4),
-                        scales=w1_scales[:, g, cols],
-                        in_=grouped[:, lo:hi, :].rearrange("p f t -> p (f t)"),
-                    )
-            if half == 0:
-                for g in range(PASSES):
-                    regroup(nc.scalar.copy, w2_grouped[:, g], w2_raw[:, PACK * g : PACK * (g + 1), :])
-                nc.vector.quantize_mx(
-                    out=w2_codes[:].rearrange("p g n -> p (g n)").bitcast(FP8X4),
-                    scales=w2_scales[:].rearrange("p g n -> p (g n)"),
-                    in_=w2_grouped[:].rearrange("p g n t -> p (g n t)"),
-                )
-
-            h_acc = psum.tile([P, PACK, TOKENS], F32, name="h_acc%d" % half)
+        def first_layer(half):
             for t in range(PACK):
                 cols = slice(half * F_HALF + t * F_TILE, half * F_HALF + (t + 1) * F_TILE)
                 for g in range(PASSES):
                     nc.tensor.matmul_mx(
-                        out=h_acc[:, t, :],
+                        out=h_acc[half][:, t, :],
                         lhsT=w1_codes[:, g, cols].bitcast(FP8X4),
                         lhsT_scale=w1_scales[:, g, cols],
                         rhs=p_codes[:, g, :].bitcast(FP8X4),
@@ -123,20 +139,18 @@ def tile_mlpconv2d_pa_s_kernel(tc, x, w1, b1, w2, b2, out):
                         start=(g == 0),
                         stop=(g == PASSES - 1),
                     )
-            h_biased = stream.tile([P, TOKENS, PACK], BF16, name="h_biased")
+
+        def hidden(half):
             nc.vector.tensor_tensor(
-                out=h_biased[:],
-                in0=h_acc[:].rearrange("p t r -> p r t"),
-                in1=b1_cols[:, PACK * half : PACK * (half + 1)].unsqueeze(1).to_broadcast([P, TOKENS, PACK]),
-                op=mybir.AluOpType.add,
+                out=h_biased[:, half],
+                in0=h_acc[half][:].rearrange("p t r -> p r t"),
+                in1=bias_cols[:, PACK * half : PACK * (half + 1)].unsqueeze(1).to_broadcast([P, TOKENS, PACK]),
+                op=ADD,
             )
-            h_grouped = stream.tile([P, TOKENS, PACK], BF16, align_bytes=64, name="h_grouped")
-            nc.vector.tensor_scalar_max(out=h_grouped[:], in0=h_biased[:], scalar1=0.0)
-            nc.vector.quantize_mx(
-                out=h_codes[:, half, :].bitcast(FP8X4),
-                scales=h_scales[:, half, :],
-                in_=h_grouped[:].rearrange("p r t -> p (r t)"),
-            )
+            nc.vector.tensor_scalar_max(out=h_grouped[:, half], in0=h_biased[:, half], scalar1=0.0)
+            quantise(h_codes[:, half, :], h_scales[:, half, :], h_grouped[:, half].rearrange("p r t -> p (r t)"))
+
+        def second_layer(half):
             nc.tensor.matmul_mx(
                 out=out_acc[:],
                 lhsT=h_codes[:, half, :].bitcast(FP8X4),
@@ -144,11 +158,29 @@ def tile_mlpconv2d_pa_s_kernel(tc, x, w1, b1, w2, b2, out):
                 rhs=w2_codes[:, half, :].bitcast(FP8X4),
                 rhs_scale=w2_scales[:, half, :],
                 start=(half == 0),
-                stop=(half == 1),
+                stop=(half == HALVES - 1),
             )
 
+        prepare_w1(0)
+        turn_biases()
+        first_layer(0)
+        hidden(0)
+        prepare_w1(1)
+        for g in range(PASSES):
+            regroup(nc.scalar.copy, w2_grouped[:, g], w2_raw[:, g])
+        nc.scalar.copy(out=b2_all[:], in_=b2_spread[:])
+        first_layer(1)
+        quantise(
+            w2_codes[:].rearrange("p g n -> p (g n)"),
+            w2_scales[:].rearrange("p g n -> p (g n)"),
+            w2_grouped[:].rearrange("p g n t -> p (g n t)"),
+        )
+        second_layer(0)
+        hidden(1)
+        second_layer(1)
+
         biased = keep.tile([P, F2], F32)
-        nc.vector.tensor_tensor(out=biased[:], in0=out_acc[:], in1=b2_all[:], op=mybir.AluOpType.add)
+        nc.vector.tensor_tensor(out=biased[:], in0=out_acc[:], in1=b2_all[:], op=ADD)
         result = keep.tile([P, F2], F32)
         nc.vector.tensor_scalar_max(out=result[:], in0=biased[:], scalar1=0.0)
         nc.sync.dma_start(out=out.flatten_outer_dims(), in_=result[:])

@@ -24,7 +24,6 @@ ROWS_KEPT = STRIDE * (GRID - 1) + 1
 RUN = ROWS_KEPT * WIDTH
 U_STEP = STRIDE * WIDTH
 B1_ROWS = F1 // P
-QUANT_COLS = 256
 VECTOR_COLS = 256
 
 FLOPS = 2 * TOKENS * 1024 * F1 + 2 * TOKENS * F1 * F2
@@ -39,83 +38,27 @@ def regroup(copy, grouped, raw):
 
 def tile_mlpconv2d_pa_s_kernel(tc, x, w1, b1, w2, b2, out):
     nc = tc.nc
-    with tc.tile_pool(name="keep", bufs=1) as keep, tc.psum_pool(name="psum", bufs=1) as psum:
+    with tc.tile_pool(name="keep", bufs=1) as keep, tc.psum_pool(name="psum", bufs=1) as psum, tc.manual_schedule():
 
         def quantise(codes, scales, grouped):
             nc.vector.quantize_mx(out=codes.bitcast(FP8X4), scales=scales, in_=grouped)
 
         rows = keep.tile([P, IMAGES, GRID * U_STEP], BF16)
-        for i in range(WINDOW):
-            queue = nc.scalar if i < 6 else nc.gpsimd
-            queue.dma_start(
-                out=rows[i:P:WINDOW, :, 0:RUN],
-                in_=x[:, :, i : i + ROWS_KEPT, :].rearrange("n c h w -> c n (h w)"),
-            )
         bias_rows = keep.tile([P, P], BF16)
-        nc.vector.memset(bias_rows[:], 0.0)
-        w1_view = w1.rearrange("(p g t) f -> p g t f", g=PASSES, t=PACK)
+        warm = keep.tile([P, 2], F32)
         w1_raw = keep.tile([P, HALVES, PASSES, PACK, F_HALF], BF16)
-        for half in range(HALVES):
-            for g in range(PASSES):
-                nc.sync.dma_start(out=w1_raw[:, half, g], in_=w1_view[:, g, :, half * F_HALF : (half + 1) * F_HALF])
-            if half == 0:
-                nc.sync.dma_start(out=bias_rows[0:B1_ROWS, :], in_=b1.rearrange("(m p) -> m p", p=P))
-                nc.sync.dma_start(out=bias_rows[B1_ROWS : B1_ROWS + 1, :], in_=b2.unsqueeze(0))
         w2_raw = keep.tile([P, PASSES, PACK, F2], BF16)
-        nc.sync.dma_start(out=w2_raw[:], in_=w2.rearrange("(g t p) n -> p g t n", t=PACK, p=P))
-
         p_grouped = keep.tile([P, PASSES, TOKENS, PACK], BF16, align_bytes=64)
         p_codes = keep.tile([P, PASSES, TOKENS], U32, align_bytes=64)
         p_scales = keep.tile([P, PASSES, TOKENS], U8, align_bytes=64)
-        by_grid_row = rows[:].rearrange("p n (u r) -> p (n u) r", r=U_STEP)
-        for g in range(PASSES):
-            copy = nc.vector.tensor_copy if g == 0 else nc.scalar.copy
-            pairs = p_grouped[:, g].rearrange("p (a v) (h e) -> p h a v e", v=GRID, e=2)
-            for h in range(2):
-                first = PACK * g + 2 * h
-                copy(
-                    out=pairs[:, h],
-                    in_=by_grid_row[:, :, first : first + 2 * GRID].rearrange("p a (v e) -> p a v e", e=2),
-                )
-        for g in range(PASSES):
-            quantise(p_codes[:, g, :], p_scales[:, g, :], p_grouped[:, g].rearrange("p r t -> p (r t)"))
-
         w1_grouped = keep.tile([P, HALVES, PASSES, F_HALF, PACK], BF16, align_bytes=64)
         w1_codes = keep.tile([P, PASSES, F1], U32, align_bytes=64)
         w1_scales = keep.tile([P, PASSES, F1], U8, align_bytes=64)
-
-        def prepare_w1(half):
-            for g in range(PASSES):
-                raw = w1_raw[:, half, g]
-                grouped = w1_grouped[:, half, g]
-                regroup(nc.vector.tensor_copy, grouped[:, 0:VECTOR_COLS, :], raw[:, :, 0:VECTOR_COLS])
-                regroup(nc.scalar.copy, grouped[:, VECTOR_COLS:F_HALF, :], raw[:, :, VECTOR_COLS:F_HALF])
-                for lo in range(0, F_HALF, QUANT_COLS):
-                    cols = slice(half * F_HALF + lo, half * F_HALF + lo + QUANT_COLS)
-                    quantise(
-                        w1_codes[:, g, cols],
-                        w1_scales[:, g, cols],
-                        grouped[:, lo : lo + QUANT_COLS, :].rearrange("p f t -> p (f t)"),
-                    )
-
         ident = keep.tile([P, P], BF16)
-        make_identity(nc, ident[:])
         bias_turned = psum.tile([P, P], BF16)
         bias_cols = keep.tile([P, B1_ROWS + 1], BF16)
         b2_spread = psum.tile([P, F2], F32)
         b2_all = keep.tile([P, F2], F32)
-
-        def turn_biases():
-            nc.tensor.transpose(out=bias_turned[:], in_=bias_rows[:], identity=ident[:])
-            nc.vector.tensor_copy(out=bias_cols[:], in_=bias_turned[:, 0 : B1_ROWS + 1])
-            nc.tensor.matmul(
-                out=b2_spread[:],
-                lhsT=bias_cols[:, B1_ROWS : B1_ROWS + 1].to_broadcast([P, P]),
-                rhs=ident[:],
-                start=True,
-                stop=True,
-            )
-
         h_acc = [psum.tile([P, PACK, TOKENS], F32, name="h_acc%d" % half) for half in range(HALVES)]
         h_biased = keep.tile([P, HALVES, TOKENS, PACK], BF16)
         h_grouped = keep.tile([P, HALVES, TOKENS, PACK], BF16, align_bytes=64)
@@ -125,6 +68,59 @@ def tile_mlpconv2d_pa_s_kernel(tc, x, w1, b1, w2, b2, out):
         w2_codes = keep.tile([P, PASSES, F2], U32, align_bytes=64)
         w2_scales = keep.tile([P, PASSES, F2], U8, align_bytes=64)
         out_acc = psum.tile([P, F2], F32)
+        biased = keep.tile([P, F2], F32)
+        result = keep.tile([P, F2], F32)
+
+        def load_x(queue, i):
+            queue.dma_start(
+                out=rows[i:P:WINDOW, :, 0:RUN],
+                in_=x[:, :, i : i + ROWS_KEPT, :].rearrange("n c h w -> c n (h w)"),
+            )
+
+        w1_view = w1.rearrange("(p g t) f -> p g t f", g=PASSES, t=PACK)
+
+        def load_w1(half, g):
+            nc.sync.dma_start(out=w1_raw[:, half, g], in_=w1_view[:, g, :, half * F_HALF : (half + 1) * F_HALF])
+
+        nc.gpsimd.memset(warm[:, 0:1], 0.0)
+        nc.gpsimd.memset(bias_rows[:], 0.0)
+        for i in range(4):
+            load_x(nc.scalar, i)
+        load_w1(0, 0)
+        load_w1(0, 1)
+        load_x(nc.sync, 4)
+        load_x(nc.sync, 5)
+        load_x(nc.gpsimd, 6)
+        load_x(nc.gpsimd, 7)
+        load_w1(1, 0)
+        load_w1(1, 1)
+        nc.sync.dma_start(out=bias_rows[0:B1_ROWS, :], in_=b1.rearrange("(m p) -> m p", p=P))
+        nc.sync.dma_start(out=bias_rows[B1_ROWS : B1_ROWS + 1, :], in_=b2.unsqueeze(0))
+        nc.sync.dma_start(out=w2_raw[:], in_=w2.rearrange("(g t p) n -> p g t n", t=PACK, p=P))
+        make_identity(nc, ident[:])
+        nc.scalar.copy(out=warm[:, 1:2], in_=warm[:, 0:1])
+
+        by_grid_row = rows[:].rearrange("p n (u r) -> p (n u) r", r=U_STEP)
+
+        def gather_p(copy, g):
+            pairs = p_grouped[:, g].rearrange("p (a v) (h e) -> p h a v e", v=GRID, e=2)
+            for h in range(2):
+                first = PACK * g + 2 * h
+                copy(
+                    out=pairs[:, h],
+                    in_=by_grid_row[:, :, first : first + 2 * GRID].rearrange("p a (v e) -> p a v e", e=2),
+                )
+
+        def regroup_w1(copy, half, g, lo, hi):
+            regroup(copy, w1_grouped[:, half, g, lo:hi, :], w1_raw[:, half, g, :, lo:hi])
+
+        def quantise_w1(half, g, lo, hi):
+            cols = slice(half * F_HALF + lo, half * F_HALF + hi)
+            quantise(
+                w1_codes[:, g, cols],
+                w1_scales[:, g, cols],
+                w1_grouped[:, half, g, lo:hi, :].rearrange("p f t -> p (f t)"),
+            )
 
         def first_layer(half):
             for t in range(PACK):
@@ -161,15 +157,48 @@ def tile_mlpconv2d_pa_s_kernel(tc, x, w1, b1, w2, b2, out):
                 stop=(half == HALVES - 1),
             )
 
-        prepare_w1(0)
-        turn_biases()
+        V = VECTOR_COLS
+        vcopy = nc.vector.tensor_copy
+        scopy = nc.scalar.copy
+
+        regroup_w1(vcopy, 0, 0, 0, V)
+        regroup_w1(scopy, 0, 0, V, F_HALF)
+        quantise_w1(0, 0, 0, V)
+        regroup_w1(vcopy, 0, 1, 0, V)
+        regroup_w1(scopy, 0, 1, V, F_HALF)
+        quantise_w1(0, 0, V, F_HALF)
+        quantise_w1(0, 1, 0, V)
+        gather_p(vcopy, 0)
+        gather_p(scopy, 1)
+        regroup_w1(vcopy, 1, 0, 0, V)
+        regroup_w1(scopy, 1, 0, V, F_HALF)
+        quantise(
+            p_codes[:].rearrange("p g r -> p (g r)"),
+            p_scales[:].rearrange("p g r -> p (g r)"),
+            p_grouped[:].rearrange("p g r t -> p (g r t)"),
+        )
+        quantise_w1(0, 1, V, F_HALF)
         first_layer(0)
-        hidden(0)
-        prepare_w1(1)
-        for g in range(PASSES):
-            regroup(nc.scalar.copy, w2_grouped[:, g], w2_raw[:, g])
-        nc.scalar.copy(out=b2_all[:], in_=b2_spread[:])
+        quantise_w1(1, 0, 0, V)
+        regroup_w1(vcopy, 1, 1, 0, V)
+        regroup_w1(scopy, 1, 1, V, F_HALF)
+        quantise_w1(1, 0, V, F_HALF)
+        quantise_w1(1, 1, 0, V)
+        quantise_w1(1, 1, V, F_HALF)
+        nc.tensor.transpose(out=bias_turned[:], in_=bias_rows[:], identity=ident[:])
+        nc.scalar.copy(out=bias_cols[:], in_=bias_turned[:, 0 : B1_ROWS + 1])
         first_layer(1)
+        nc.tensor.matmul(
+            out=b2_spread[:],
+            lhsT=bias_cols[:, B1_ROWS : B1_ROWS + 1].to_broadcast([P, P]),
+            rhs=ident[:],
+            start=True,
+            stop=True,
+        )
+        for g in range(PASSES):
+            regroup(scopy, w2_grouped[:, g], w2_raw[:, g])
+        nc.scalar.copy(out=b2_all[:], in_=b2_spread[:])
+        hidden(0)
         quantise(
             w2_codes[:].rearrange("p g n -> p (g n)"),
             w2_scales[:].rearrange("p g n -> p (g n)"),
@@ -179,8 +208,6 @@ def tile_mlpconv2d_pa_s_kernel(tc, x, w1, b1, w2, b2, out):
         hidden(1)
         second_layer(1)
 
-        biased = keep.tile([P, F2], F32)
         nc.vector.tensor_tensor(out=biased[:], in0=out_acc[:], in1=b2_all[:], op=ADD)
-        result = keep.tile([P, F2], F32)
         nc.vector.tensor_scalar_max(out=result[:], in0=biased[:], scalar1=0.0)
         nc.sync.dma_start(out=out.flatten_outer_dims(), in_=result[:])

@@ -7,6 +7,7 @@ U32 = mybir.dt.uint32
 U8 = mybir.dt.uint8
 FP8X4 = mybir.dt.float8_e4m3fn_x4
 ADD = mybir.AluOpType.add
+RELU = mybir.ActivationFunctionType.Relu
 
 P = 128
 PACK = 4
@@ -59,8 +60,9 @@ def tile_mlpconv2d_pa_s_kernel(tc, x, w1, b1, w2, b2, out):
         bias_cols = keep.tile([P, B1_ROWS + 1], BF16)
         b2_spread = psum.tile([P, F2], F32)
         b2_all = keep.tile([P, F2], F32)
-        h_acc = [psum.tile([P, PACK, TOKENS], F32, name="h_acc%d" % half) for half in range(HALVES)]
-        h_biased = keep.tile([P, HALVES, TOKENS, PACK], BF16)
+        h_acc0 = psum.tile([P, PACK, TOKENS], F32)
+        h_acc1 = [psum.tile([P, TOKENS], F32, name="h_acc1_%d" % t) for t in range(PACK)]
+        h_relu = keep.tile([P, HALVES, PACK, TOKENS], BF16)
         h_grouped = keep.tile([P, HALVES, TOKENS, PACK], BF16, align_bytes=64)
         h_codes = keep.tile([P, HALVES, TOKENS], U32, align_bytes=64)
         h_scales = keep.tile([P, HALVES, TOKENS], U8, align_bytes=64)
@@ -122,29 +124,37 @@ def tile_mlpconv2d_pa_s_kernel(tc, x, w1, b1, w2, b2, out):
                 w1_grouped[:, half, g, lo:hi, :].rearrange("p f t -> p (f t)"),
             )
 
-        def first_layer(half):
-            for t in range(PACK):
-                cols = slice(half * F_HALF + t * F_TILE, half * F_HALF + (t + 1) * F_TILE)
-                for g in range(PASSES):
-                    nc.tensor.matmul_mx(
-                        out=h_acc[half][:, t, :],
-                        lhsT=w1_codes[:, g, cols].bitcast(FP8X4),
-                        lhsT_scale=w1_scales[:, g, cols],
-                        rhs=p_codes[:, g, :].bitcast(FP8X4),
-                        rhs_scale=p_scales[:, g, :],
-                        start=(g == 0),
-                        stop=(g == PASSES - 1),
-                    )
+        def h_sum(half, t):
+            return h_acc0[:, t, :] if half == 0 else h_acc1[t][:]
 
-        def hidden(half):
-            nc.vector.tensor_tensor(
-                out=h_biased[:, half],
-                in0=h_acc[half][:].rearrange("p t r -> p r t"),
-                in1=bias_cols[:, PACK * half : PACK * (half + 1)].unsqueeze(1).to_broadcast([P, TOKENS, PACK]),
-                op=ADD,
+        def first_layer(half, t, g):
+            cols = slice(half * F_HALF + t * F_TILE, half * F_HALF + (t + 1) * F_TILE)
+            nc.tensor.matmul_mx(
+                out=h_sum(half, t),
+                lhsT=w1_codes[:, g, cols].bitcast(FP8X4),
+                lhsT_scale=w1_scales[:, g, cols],
+                rhs=p_codes[:, g, :].bitcast(FP8X4),
+                rhs_scale=p_scales[:, g, :],
+                start=(g == 0),
+                stop=(g == PASSES - 1),
             )
-            nc.vector.tensor_scalar_max(out=h_grouped[:, half], in0=h_biased[:, half], scalar1=0.0)
+
+        def bias_relu(half, t):
+            m = PACK * half + t
+            nc.scalar.activation(out=h_relu[:, half, t, :], in_=h_sum(half, t), func=RELU, bias=bias_cols[:, m : m + 1])
+
+        def group_h(half):
+            regroup(vcopy, h_grouped[:, half], h_relu[:, half])
+
+        def quantise_h(half):
             quantise(h_codes[:, half, :], h_scales[:, half, :], h_grouped[:, half].rearrange("p r t -> p (r t)"))
+
+        def quantise_w2():
+            quantise(
+                w2_codes[:].rearrange("p g n -> p (g n)"),
+                w2_scales[:].rearrange("p g n -> p (g n)"),
+                w2_grouped[:].rearrange("p g n t -> p (g n t)"),
+            )
 
         def second_layer(half):
             nc.tensor.matmul_mx(
@@ -178,16 +188,30 @@ def tile_mlpconv2d_pa_s_kernel(tc, x, w1, b1, w2, b2, out):
             p_grouped[:].rearrange("p g r t -> p (g r t)"),
         )
         quantise_w1(0, 1, V, F_HALF)
-        first_layer(0)
+        for t in range(PACK):
+            for g in range(PASSES):
+                first_layer(0, t, g)
+        nc.tensor.transpose(out=bias_turned[:], in_=bias_rows[:], identity=ident[:])
         quantise_w1(1, 0, 0, V)
         regroup_w1(vcopy, 1, 1, 0, V)
         regroup_w1(scopy, 1, 1, V, F_HALF)
         quantise_w1(1, 0, V, F_HALF)
+        for t in range(PACK):
+            first_layer(1, t, 0)
         quantise_w1(1, 1, 0, V)
         quantise_w1(1, 1, V, F_HALF)
-        nc.tensor.transpose(out=bias_turned[:], in_=bias_rows[:], identity=ident[:])
+        for t in range(PACK):
+            first_layer(1, t, 1)
+        regroup(scopy, w2_grouped[:, 0], w2_raw[:, 0])
         nc.scalar.copy(out=bias_cols[:], in_=bias_turned[:, 0 : B1_ROWS + 1])
-        first_layer(1)
+        for t in (3, 0, 1, 2):
+            bias_relu(0, t)
+        regroup(vcopy, w2_grouped[:, 1], w2_raw[:, 1])
+        quantise_w2()
+        group_h(0)
+        for t in range(PACK):
+            bias_relu(1, t)
+        quantise_h(0)
         nc.tensor.matmul(
             out=b2_spread[:],
             lhsT=bias_cols[:, B1_ROWS : B1_ROWS + 1].to_broadcast([P, P]),
@@ -195,17 +219,10 @@ def tile_mlpconv2d_pa_s_kernel(tc, x, w1, b1, w2, b2, out):
             start=True,
             stop=True,
         )
-        for g in range(PASSES):
-            regroup(scopy, w2_grouped[:, g], w2_raw[:, g])
-        nc.scalar.copy(out=b2_all[:], in_=b2_spread[:])
-        hidden(0)
-        quantise(
-            w2_codes[:].rearrange("p g n -> p (g n)"),
-            w2_scales[:].rearrange("p g n -> p (g n)"),
-            w2_grouped[:].rearrange("p g n t -> p (g n t)"),
-        )
         second_layer(0)
-        hidden(1)
+        group_h(1)
+        nc.scalar.copy(out=b2_all[:], in_=b2_spread[:])
+        quantise_h(1)
         second_layer(1)
 
         nc.vector.tensor_tensor(out=biased[:], in0=out_acc[:], in1=b2_all[:], op=ADD)

@@ -16,6 +16,7 @@ PASSES = 2
 IMAGES, CHANNELS, HEIGHT, WIDTH = 2, 16, 22, 22
 WINDOW, STRIDE, GRID = 8, 2, 8
 TOKENS = IMAGES * GRID * GRID
+HALF_TOKENS = TOKENS // 2
 F1 = 1024
 F2 = 128
 F_TILE = 128
@@ -105,12 +106,13 @@ def tile_mlpconv2d_pa_s_kernel(tc, x, w1, b1, w2, b2, out):
         by_grid_row = rows[:].rearrange("p n (u r) -> p (n u) r", r=U_STEP)
 
         def gather_p(copy, g):
-            pairs = p_grouped[:, g].rearrange("p (a v) (h e) -> p h a v e", v=GRID, e=2)
-            for h in range(2):
-                first = PACK * g + 2 * h
+            for odd in range(2):
+                first = PACK * g + 2 * odd
                 copy(
-                    out=pairs[:, h],
-                    in_=by_grid_row[:, :, first : first + 2 * GRID].rearrange("p a (v e) -> p a v e", e=2),
+                    out=p_grouped[:, g, odd * HALF_TOKENS : (odd + 1) * HALF_TOKENS, :].rearrange(
+                        "p (a w) t -> p a (w t)", w=GRID // 2
+                    ),
+                    in_=by_grid_row[:, :, first : first + 2 * GRID],
                 )
 
         def regroup_w1(copy, half, g, lo, hi):
@@ -141,7 +143,12 @@ def tile_mlpconv2d_pa_s_kernel(tc, x, w1, b1, w2, b2, out):
 
         def bias_relu(half, t):
             m = PACK * half + t
-            nc.scalar.activation(out=h_relu[:, half, t, :], in_=h_sum(half, t), func=RELU, bias=bias_cols[:, m : m + 1])
+            nc.scalar.activation(
+                out=h_relu[:, half, t, :].rearrange("p (q odd) -> p q odd", odd=2),
+                in_=h_sum(half, t).rearrange("p (odd q) -> p q odd", odd=2),
+                func=RELU,
+                bias=bias_cols[:, m : m + 1],
+            )
 
         def group_h(half):
             regroup(vcopy, h_grouped[:, half], h_relu[:, half])

@@ -57,9 +57,9 @@ def tile_mlpconv2d_pa_s_kernel(tc, x, w1, b1, w2, b2, out):
         w1_codes = keep.tile([P, PASSES, F1], U32, align_bytes=64)
         w1_scales = keep.tile([P, PASSES, F1], U8, align_bytes=64)
         ident = keep.tile([P, P], BF16)
-        bias_turned = psum.tile([P, P], BF16)
+        bias_turned = psum.tile([P, P], BF16, tag="biases")
+        idle_sums = psum.tile([P, 2 * F_TILE], F32)
         bias_cols = keep.tile([P, B1_ROWS + 1], BF16)
-        b2_spread = psum.tile([P, F2], F32)
         b2_all = keep.tile([P, F2], F32)
         h_acc0 = psum.tile([P, PACK, TOKENS], F32)
         h_acc1 = [psum.tile([P, TOKENS], F32, name="h_acc1_%d" % t) for t in range(PACK)]
@@ -129,6 +129,22 @@ def tile_mlpconv2d_pa_s_kernel(tc, x, w1, b1, w2, b2, out):
         def h_sum(half, t):
             return h_acc0[:, t, :] if half == 0 else h_acc1[t][:]
 
+        def keep_clock_up(codes, scales):
+            for again in range(2):
+                nc.tensor.matmul_mx(
+                    out=idle_sums[:],
+                    lhsT=codes[:, 0:F_TILE].bitcast(FP8X4),
+                    lhsT_scale=scales[:, 0:F_TILE],
+                    rhs=codes.bitcast(FP8X4),
+                    rhs_scale=scales,
+                    start=True,
+                    stop=True,
+                )
+
+        def keep_clock_up_w1(half, g, lo):
+            cols = slice(half * F_HALF + lo, half * F_HALF + lo + 2 * F_TILE)
+            keep_clock_up(w1_codes[:, g, cols], w1_scales[:, g, cols])
+
         def first_layer(half, t, g):
             cols = slice(half * F_HALF + t * F_TILE, half * F_HALF + (t + 1) * F_TILE)
             nc.tensor.matmul_mx(
@@ -181,10 +197,13 @@ def tile_mlpconv2d_pa_s_kernel(tc, x, w1, b1, w2, b2, out):
         regroup_w1(vcopy, 0, 0, 0, V)
         regroup_w1(scopy, 0, 0, V, F_HALF)
         quantise_w1(0, 0, 0, V)
+        keep_clock_up_w1(0, 0, 0)
         regroup_w1(vcopy, 0, 1, 0, V)
         regroup_w1(scopy, 0, 1, V, F_HALF)
         quantise_w1(0, 0, V, F_HALF)
+        keep_clock_up_w1(0, 0, V)
         quantise_w1(0, 1, 0, V)
+        keep_clock_up_w1(0, 1, 0)
         gather_p(vcopy, 0)
         gather_p(scopy, 1)
         regroup_w1(vcopy, 1, 0, 0, V)
@@ -200,6 +219,7 @@ def tile_mlpconv2d_pa_s_kernel(tc, x, w1, b1, w2, b2, out):
                 first_layer(0, t, g)
         nc.tensor.transpose(out=bias_turned[:], in_=bias_rows[:], identity=ident[:])
         quantise_w1(1, 0, 0, V)
+        keep_clock_up_w1(1, 0, 0)
         regroup_w1(vcopy, 1, 1, 0, V)
         regroup_w1(scopy, 1, 1, V, F_HALF)
         quantise_w1(1, 0, V, F_HALF)
@@ -215,10 +235,12 @@ def tile_mlpconv2d_pa_s_kernel(tc, x, w1, b1, w2, b2, out):
             bias_relu(0, t)
         regroup(vcopy, w2_grouped[:, 1], w2_raw[:, 1])
         quantise_w2()
+        keep_clock_up(w2_codes[:].rearrange("p g n -> p (g n)"), w2_scales[:].rearrange("p g n -> p (g n)"))
         group_h(0)
         for t in range(PACK):
             bias_relu(1, t)
         quantise_h(0)
+        b2_spread = psum.tile([P, F2], F32, tag="biases")
         nc.tensor.matmul(
             out=b2_spread[:],
             lhsT=bias_cols[:, B1_ROWS : B1_ROWS + 1].to_broadcast([P, P]),

@@ -22,11 +22,11 @@ F2 = 128
 F_TILE = 128
 F_HALF = PACK * F_TILE
 HALVES = F1 // F_HALF
-ROWS_KEPT = STRIDE * (GRID - 1) + 1
-RUN = ROWS_KEPT * WIDTH
-U_STEP = STRIDE * WIDTH
+ROW_PAIRS = WINDOW // STRIDE
+ROWS_KEPT = STRIDE * GRID
 B1_ROWS = F1 // P
 VECTOR_COLS = 256
+LAST_V = 448
 
 FLOPS = 2 * TOKENS * 1024 * F1 + 2 * TOKENS * F1 * F2
 
@@ -45,7 +45,8 @@ def tile_mlpconv2d_pa_s_kernel(tc, x, w1, b1, w2, b2, out):
         def quantise(codes, scales, grouped):
             nc.vector.quantize_mx(out=codes.bitcast(FP8X4), scales=scales, in_=grouped)
 
-        rows = keep.tile([P, IMAGES, GRID * U_STEP], BF16)
+        x_rows = keep.tile([P, ROWS_KEPT * WIDTH], BF16)
+        select = keep.tile([P, IMAGES, STRIDE, P], BF16)
         bias_rows = keep.tile([P, P], BF16)
         warm = keep.tile([P, 2], F32)
         w1_raw = keep.tile([P, HALVES, PASSES, PACK, F_HALF], BF16)
@@ -57,8 +58,7 @@ def tile_mlpconv2d_pa_s_kernel(tc, x, w1, b1, w2, b2, out):
         w1_codes = keep.tile([P, PASSES, F1], U32, align_bytes=64)
         w1_scales = keep.tile([P, PASSES, F1], U8, align_bytes=64)
         ident = keep.tile([P, P], BF16)
-        bias_turned = psum.tile([P, P], BF16, tag="biases")
-        idle_sums = psum.tile([P, 2 * F_TILE], F32)
+        spread = [psum.tile([P, GRID, WIDTH], BF16, name="spread_%d" % n, tag=tag) for n, tag in enumerate(("biases", "out"))]
         bias_cols = keep.tile([P, B1_ROWS + 1], BF16)
         b2_all = keep.tile([P, F2], F32)
         h_acc0 = psum.tile([P, PACK, TOKENS], F32)
@@ -70,14 +70,13 @@ def tile_mlpconv2d_pa_s_kernel(tc, x, w1, b1, w2, b2, out):
         w2_grouped = keep.tile([P, PASSES, F2, PACK], BF16, align_bytes=64)
         w2_codes = keep.tile([P, PASSES, F2], U32, align_bytes=64)
         w2_scales = keep.tile([P, PASSES, F2], U8, align_bytes=64)
-        out_acc = psum.tile([P, F2], F32)
         biased = keep.tile([P, F2], F32)
         result = keep.tile([P, F2], F32)
 
-        def load_x(queue, i):
+        def load_x(queue, a):
             queue.dma_start(
-                out=rows[i:P:WINDOW, :, 0:RUN],
-                in_=x[:, :, i : i + ROWS_KEPT, :].rearrange("n c h w -> c n (h w)"),
+                out=x_rows[2 * CHANNELS * a : 2 * CHANNELS * (a + 1), :],
+                in_=x[:, :, STRIDE * a : STRIDE * a + ROWS_KEPT, :].rearrange("n c h w -> (n c) (h w)"),
             )
 
         w1_view = w1.rearrange("(p g t) f -> p g t f", g=PASSES, t=PACK)
@@ -87,33 +86,54 @@ def tile_mlpconv2d_pa_s_kernel(tc, x, w1, b1, w2, b2, out):
 
         nc.gpsimd.memset(warm[:, 0:1], 0.0)
         nc.gpsimd.memset(bias_rows[:], 0.0)
-        for i in range(4):
-            load_x(nc.scalar, i)
+        for a in range(ROW_PAIRS):
+            load_x(nc.scalar, a)
         load_w1(0, 0)
-        load_w1(0, 1)
-        load_x(nc.sync, 4)
-        load_x(nc.sync, 5)
-        load_x(nc.gpsimd, 6)
-        load_x(nc.gpsimd, 7)
-        load_w1(1, 0)
-        load_w1(1, 1)
         nc.sync.dma_start(out=bias_rows[0:B1_ROWS, :], in_=b1.rearrange("(m p) -> m p", p=P))
         nc.sync.dma_start(out=bias_rows[B1_ROWS : B1_ROWS + 1, :], in_=b2.unsqueeze(0))
+        load_w1(0, 1)
+        load_w1(1, 0)
+        load_w1(1, 1)
         nc.sync.dma_start(out=w2_raw[:], in_=w2.rearrange("(g t p) n -> p g t n", t=PACK, p=P))
         make_identity(nc, ident[:])
         nc.scalar.copy(out=warm[:, 1:2], in_=warm[:, 0:1])
-
-        by_grid_row = rows[:].rearrange("p n (u r) -> p (n u) r", r=U_STEP)
-
-        def gather_p(copy, g):
-            for odd in range(2):
-                first = PACK * g + 2 * odd
-                copy(
-                    out=p_grouped[:, g, odd * HALF_TOKENS : (odd + 1) * HALF_TOKENS, :].rearrange(
-                        "p (a w) t -> p a (w t)", w=GRID // 2
-                    ),
-                    in_=by_grid_row[:, :, first : first + 2 * GRID],
+        nc.vector.memset(select[:], 0.0)
+        for n in range(IMAGES):
+            for b in range(STRIDE):
+                nc.vector.tensor_copy(
+                    out=select[:, n, b].rearrange("p (c a b) -> p b c a", a=ROW_PAIRS, b=STRIDE)[:, b],
+                    in_=ident[:].rearrange("p (a n c) -> p n c a", a=ROW_PAIRS, n=IMAGES)[:, n],
                 )
+
+        def spread_x(n):
+            by_parity = x_rows[:].rearrange("p (u b w) -> p b u w", b=STRIDE, w=WIDTH)
+            for b in range(STRIDE):
+                nc.tensor.matmul(
+                    out=spread[n][:],
+                    lhsT=select[:, n, b],
+                    rhs=by_parity[:, b],
+                    start=(b == 0),
+                    stop=(b == STRIDE - 1),
+                )
+
+        def gather_p(copy, n):
+            for g in range(PASSES):
+                for odd in range(2):
+                    first = PACK * g + 2 * odd
+                    place = odd * HALF_TOKENS + n * HALF_TOKENS // 2
+                    copy(
+                        out=p_grouped[:, g, place : place + HALF_TOKENS // 2, :].rearrange(
+                            "p (u w) t -> p u (w t)", w=GRID // 2
+                        ),
+                        in_=spread[n][:, :, first : first + 2 * GRID],
+                    )
+
+        def quantise_p():
+            quantise(
+                p_codes[:].rearrange("p g r -> p (g r)"),
+                p_scales[:].rearrange("p g r -> p (g r)"),
+                p_grouped[:].rearrange("p g r t -> p (g r t)"),
+            )
 
         def regroup_w1(copy, half, g, lo, hi):
             regroup(copy, w1_grouped[:, half, g, lo:hi, :], w1_raw[:, half, g, :, lo:hi])
@@ -128,22 +148,6 @@ def tile_mlpconv2d_pa_s_kernel(tc, x, w1, b1, w2, b2, out):
 
         def h_sum(half, t):
             return h_acc0[:, t, :] if half == 0 else h_acc1[t][:]
-
-        def keep_clock_up(codes, scales):
-            for again in range(2):
-                nc.tensor.matmul_mx(
-                    out=idle_sums[:],
-                    lhsT=codes[:, 0:F_TILE].bitcast(FP8X4),
-                    lhsT_scale=scales[:, 0:F_TILE],
-                    rhs=codes.bitcast(FP8X4),
-                    rhs_scale=scales,
-                    start=True,
-                    stop=True,
-                )
-
-        def keep_clock_up_w1(half, g, lo):
-            cols = slice(half * F_HALF + lo, half * F_HALF + lo + 2 * F_TILE)
-            keep_clock_up(w1_codes[:, g, cols], w1_scales[:, g, cols])
 
         def first_layer(half, t, g):
             cols = slice(half * F_HALF + t * F_TILE, half * F_HALF + (t + 1) * F_TILE)
@@ -194,52 +198,51 @@ def tile_mlpconv2d_pa_s_kernel(tc, x, w1, b1, w2, b2, out):
         vcopy = nc.vector.tensor_copy
         scopy = nc.scalar.copy
 
+        for n in range(IMAGES):
+            spread_x(n)
         regroup_w1(vcopy, 0, 0, 0, V)
         regroup_w1(scopy, 0, 0, V, F_HALF)
-        quantise_w1(0, 0, 0, V)
-        keep_clock_up_w1(0, 0, 0)
-        regroup_w1(vcopy, 0, 1, 0, V)
-        regroup_w1(scopy, 0, 1, V, F_HALF)
-        quantise_w1(0, 0, V, F_HALF)
-        keep_clock_up_w1(0, 0, V)
-        quantise_w1(0, 1, 0, V)
-        keep_clock_up_w1(0, 1, 0)
         gather_p(vcopy, 0)
         gather_p(scopy, 1)
+        quantise_w1(0, 0, 0, V)
+        bias_turned = psum.tile([P, P], BF16, tag="biases")
+        nc.tensor.transpose(out=bias_turned[:], in_=bias_rows[:], identity=ident[:])
+        regroup_w1(vcopy, 0, 1, 0, V)
+        regroup_w1(scopy, 0, 1, V, F_HALF)
+        quantise_p()
+        nc.scalar.copy(out=bias_cols[:], in_=bias_turned[:, 0 : B1_ROWS + 1])
+        quantise_w1(0, 0, V, F_HALF)
+        quantise_w1(0, 1, 0, V)
         regroup_w1(vcopy, 1, 0, 0, V)
         regroup_w1(scopy, 1, 0, V, F_HALF)
-        quantise(
-            p_codes[:].rearrange("p g r -> p (g r)"),
-            p_scales[:].rearrange("p g r -> p (g r)"),
-            p_grouped[:].rearrange("p g r t -> p (g r t)"),
-        )
         quantise_w1(0, 1, V, F_HALF)
         for t in range(PACK):
             for g in range(PASSES):
                 first_layer(0, t, g)
-        nc.tensor.transpose(out=bias_turned[:], in_=bias_rows[:], identity=ident[:])
         quantise_w1(1, 0, 0, V)
-        keep_clock_up_w1(1, 0, 0)
+        first_layer(1, 0, 0)
+        first_layer(1, 1, 0)
         regroup_w1(vcopy, 1, 1, 0, V)
-        regroup_w1(scopy, 1, 1, V, F_HALF)
+        regroup_w1(scopy, 1, 1, V, LAST_V)
         quantise_w1(1, 0, V, F_HALF)
-        for t in range(PACK):
-            first_layer(1, t, 0)
+        first_layer(1, 2, 0)
+        first_layer(1, 3, 0)
+        regroup_w1(vcopy, 1, 1, LAST_V, F_HALF)
         quantise_w1(1, 1, 0, V)
+        first_layer(1, 0, 1)
+        first_layer(1, 1, 1)
         quantise_w1(1, 1, V, F_HALF)
-        for t in range(PACK):
-            first_layer(1, t, 1)
-        regroup(scopy, w2_grouped[:, 0], w2_raw[:, 0])
-        nc.scalar.copy(out=bias_cols[:], in_=bias_turned[:, 0 : B1_ROWS + 1])
+        first_layer(1, 2, 1)
+        first_layer(1, 3, 1)
         for t in (3, 0, 1, 2):
             bias_relu(0, t)
+        regroup(scopy, w2_grouped[:, 0], w2_raw[:, 0])
         regroup(vcopy, w2_grouped[:, 1], w2_raw[:, 1])
-        quantise_w2()
-        keep_clock_up(w2_codes[:].rearrange("p g n -> p (g n)"), w2_scales[:].rearrange("p g n -> p (g n)"))
         group_h(0)
+        quantise_w2()
+        quantise_h(0)
         for t in range(PACK):
             bias_relu(1, t)
-        quantise_h(0)
         b2_spread = psum.tile([P, F2], F32, tag="biases")
         nc.tensor.matmul(
             out=b2_spread[:],
@@ -248,6 +251,7 @@ def tile_mlpconv2d_pa_s_kernel(tc, x, w1, b1, w2, b2, out):
             start=True,
             stop=True,
         )
+        out_acc = psum.tile([P, F2], F32, tag="out")
         second_layer(0)
         group_h(1)
         nc.scalar.copy(out=b2_all[:], in_=b2_spread[:])

@@ -16,7 +16,8 @@ PASSES = 2
 IMAGES, CHANNELS, HEIGHT, WIDTH = 2, 16, 22, 22
 WINDOW, STRIDE, GRID = 8, 2, 8
 TOKENS = IMAGES * GRID * GRID
-HALF_TOKENS = TOKENS // 2
+GRID_ROWS = IMAGES * GRID
+WORDS = GRID + PASSES
 F1 = 1024
 F2 = 128
 F_TILE = 128
@@ -51,7 +52,7 @@ def tile_mlpconv2d_pa_s_kernel(tc, x, w1, b1, w2, b2, out):
         warm = keep.tile([P, 2], F32)
         w1_raw = keep.tile([P, HALVES, PASSES, PACK, F_HALF], BF16)
         w2_raw = keep.tile([P, PASSES, PACK, F2], BF16)
-        p_grouped = keep.tile([P, PASSES, TOKENS, PACK], BF16, align_bytes=64)
+        p_grouped = keep.tile([P, WORDS, GRID_ROWS, PACK], BF16, align_bytes=64)
         p_codes = keep.tile([P, PASSES, TOKENS], U32, align_bytes=64)
         p_scales = keep.tile([P, PASSES, TOKENS], U8, align_bytes=64)
         w1_grouped = keep.tile([P, HALVES, PASSES, F_HALF, PACK], BF16, align_bytes=64)
@@ -117,23 +118,17 @@ def tile_mlpconv2d_pa_s_kernel(tc, x, w1, b1, w2, b2, out):
                 )
 
         def gather_p(copy, n):
-            for g in range(PASSES):
-                for odd in range(2):
-                    first = PACK * g + 2 * odd
-                    place = odd * HALF_TOKENS + n * HALF_TOKENS // 2
-                    copy(
-                        out=p_grouped[:, g, place : place + HALF_TOKENS // 2, :].rearrange(
-                            "p (u w) t -> p u (w t)", w=GRID // 2
-                        ),
-                        in_=spread[n][:, :, first : first + 2 * GRID],
-                    )
+            for odd in range(2):
+                copy(
+                    out=p_grouped[:].rearrange("p (s odd) a t -> p odd s a t", odd=2)[:, odd, :, n * GRID : (n + 1) * GRID],
+                    in_=spread[n][:, :, 2 * odd : 2 * odd + 2 * WORDS].rearrange("p u (s t) -> p s u t", t=PACK),
+                )
 
         def quantise_p():
-            quantise(
-                p_codes[:].rearrange("p g r -> p (g r)"),
-                p_scales[:].rearrange("p g r -> p (g r)"),
-                p_grouped[:].rearrange("p g r t -> p (g r t)"),
-            )
+            for g in range(PASSES):
+                quantise(
+                    p_codes[:, g], p_scales[:, g], p_grouped[:, 2 * g : 2 * g + GRID].rearrange("p s a t -> p (s a t)")
+                )
 
         def regroup_w1(copy, half, g, lo, hi):
             regroup(copy, w1_grouped[:, half, g, lo:hi, :], w1_raw[:, half, g, :, lo:hi])
@@ -164,17 +159,19 @@ def tile_mlpconv2d_pa_s_kernel(tc, x, w1, b1, w2, b2, out):
         def bias_relu(half, t):
             m = PACK * half + t
             nc.scalar.activation(
-                out=h_relu[:, half, t, :].rearrange("p (q odd) -> p q odd", odd=2),
-                in_=h_sum(half, t).rearrange("p (odd q) -> p q odd", odd=2),
+                out=h_relu[:, half, t, :].rearrange("p (a v) -> p a v", v=GRID),
+                in_=h_sum(half, t).rearrange("p (v a) -> p a v", v=GRID),
                 func=RELU,
                 bias=bias_cols[:, m : m + 1],
             )
 
-        def group_h(half):
-            regroup(vcopy, h_grouped[:, half], h_relu[:, half])
+        def group_h(half, lo=0, hi=TOKENS):
+            regroup(vcopy, h_grouped[:, half, lo:hi], h_relu[:, half, :, lo:hi])
 
-        def quantise_h(half):
-            quantise(h_codes[:, half, :], h_scales[:, half, :], h_grouped[:, half].rearrange("p r t -> p (r t)"))
+        def quantise_h(half, lo=0, hi=TOKENS):
+            quantise(
+                h_codes[:, half, lo:hi], h_scales[:, half, lo:hi], h_grouped[:, half, lo:hi].rearrange("p r t -> p (r t)")
+            )
 
         def quantise_w2():
             quantise(
@@ -231,9 +228,9 @@ def tile_mlpconv2d_pa_s_kernel(tc, x, w1, b1, w2, b2, out):
         quantise_w1(1, 1, 0, V)
         first_layer(1, 0, 1)
         first_layer(1, 1, 1)
-        quantise_w1(1, 1, V, F_HALF)
-        first_layer(1, 2, 1)
-        first_layer(1, 3, 1)
+        for t in (2, 3):
+            quantise_w1(1, 1, t * F_TILE, (t + 1) * F_TILE)
+            first_layer(1, t, 1)
         for t in (3, 0, 1, 2):
             bias_relu(0, t)
         regroup(scopy, w2_grouped[:, 0], w2_raw[:, 0])
@@ -253,11 +250,17 @@ def tile_mlpconv2d_pa_s_kernel(tc, x, w1, b1, w2, b2, out):
         )
         out_acc = psum.tile([P, F2], F32, tag="out")
         second_layer(0)
-        group_h(1)
         nc.scalar.copy(out=b2_all[:], in_=b2_spread[:])
-        quantise_h(1)
+        for step in (group_h, quantise_h):
+            for lo in (0, TOKENS // 2):
+                step(1, lo, lo + TOKENS // 2)
         second_layer(1)
 
-        nc.vector.tensor_tensor(out=biased[:], in0=out_acc[:], in1=b2_all[:], op=ADD)
-        nc.vector.tensor_scalar_max(out=result[:], in0=biased[:], scalar1=0.0)
+        for step in range(2):
+            for lo in (0, F2 // 2):
+                cols = slice(lo, lo + F2 // 2)
+                if step == 0:
+                    nc.vector.tensor_tensor(out=biased[:, cols], in0=out_acc[:, cols], in1=b2_all[:, cols], op=ADD)
+                else:
+                    nc.vector.tensor_scalar_max(out=result[:, cols], in0=biased[:, cols], scalar1=0.0)
         nc.sync.dma_start(out=out.flatten_outer_dims(), in_=result[:])

@@ -71,6 +71,7 @@ def tile_mlpconv2d_pa_s_kernel(tc, x, w1, b1, w2, b2, out):
         w2_grouped = keep.tile([P, PASSES, F2, PACK], BF16, align_bytes=64)
         w2_codes = keep.tile([P, PASSES, F2], U32, align_bytes=64)
         w2_scales = keep.tile([P, PASSES, F2], U8, align_bytes=64)
+        idle_sums = psum.tile([P, 2 * F_TILE], F32)
         biased = keep.tile([P, F2], F32)
         result = keep.tile([P, F2], F32)
 
@@ -144,6 +145,19 @@ def tile_mlpconv2d_pa_s_kernel(tc, x, w1, b1, w2, b2, out):
         def h_sum(half, t):
             return h_acc0[:, t, :] if half == 0 else h_acc1[t][:]
 
+        def keep_clock_up(half, g, passes):
+            cols = slice(half * F_HALF, half * F_HALF + 2 * F_TILE)
+            for again in range(passes):
+                nc.tensor.matmul_mx(
+                    out=idle_sums[:],
+                    lhsT=w1_codes[:, g, half * F_HALF : half * F_HALF + F_TILE].bitcast(FP8X4),
+                    lhsT_scale=w1_scales[:, g, half * F_HALF : half * F_HALF + F_TILE],
+                    rhs=w1_codes[:, g, cols].bitcast(FP8X4),
+                    rhs_scale=w1_scales[:, g, cols],
+                    start=True,
+                    stop=True,
+                )
+
         def first_layer(half, t, g):
             cols = slice(half * F_HALF + t * F_TILE, half * F_HALF + (t + 1) * F_TILE)
             nc.tensor.matmul_mx(
@@ -208,6 +222,7 @@ def tile_mlpconv2d_pa_s_kernel(tc, x, w1, b1, w2, b2, out):
         regroup_w1(scopy, 0, 1, V, F_HALF)
         quantise_p()
         nc.scalar.copy(out=bias_cols[:], in_=bias_turned[:, 0 : B1_ROWS + 1])
+        keep_clock_up(0, 0, 4)
         quantise_w1(0, 0, V, F_HALF)
         quantise_w1(0, 1, 0, V)
         regroup_w1(vcopy, 1, 0, 0, V)
@@ -216,14 +231,17 @@ def tile_mlpconv2d_pa_s_kernel(tc, x, w1, b1, w2, b2, out):
         for t in range(PACK):
             for g in range(PASSES):
                 first_layer(0, t, g)
+        keep_clock_up(0, 1, 1)
         quantise_w1(1, 0, 0, V)
         first_layer(1, 0, 0)
         first_layer(1, 1, 0)
+        keep_clock_up(1, 0, 2)
         regroup_w1(vcopy, 1, 1, 0, V)
         regroup_w1(scopy, 1, 1, V, LAST_V)
         quantise_w1(1, 0, V, F_HALF)
         first_layer(1, 2, 0)
         first_layer(1, 3, 0)
+        keep_clock_up(1, 0, 1)
         regroup_w1(vcopy, 1, 1, LAST_V, F_HALF)
         quantise_w1(1, 1, 0, V)
         first_layer(1, 0, 1)
@@ -250,6 +268,7 @@ def tile_mlpconv2d_pa_s_kernel(tc, x, w1, b1, w2, b2, out):
         )
         out_acc = psum.tile([P, F2], F32, tag="out")
         second_layer(0)
+        keep_clock_up(1, 1, 2)
         nc.scalar.copy(out=b2_all[:], in_=b2_spread[:])
         for step in (group_h, quantise_h):
             for lo in (0, TOKENS // 2):

@@ -16,8 +16,7 @@ PASSES = 2
 IMAGES, CHANNELS, HEIGHT, WIDTH = 2, 16, 22, 22
 WINDOW, STRIDE, GRID = 8, 2, 8
 TOKENS = IMAGES * GRID * GRID
-GRID_ROWS = IMAGES * GRID
-WORDS = GRID + PASSES
+HALF_TOKENS = TOKENS // 2
 F1 = 1024
 F2 = 128
 F_TILE = 128
@@ -52,7 +51,7 @@ def tile_mlpconv2d_pa_s_kernel(tc, x, w1, b1, w2, b2, out):
         warm = keep.tile([P, 2], F32)
         w1_raw = keep.tile([P, HALVES, PASSES, PACK, F_HALF], BF16)
         w2_raw = keep.tile([P, PASSES, PACK, F2], BF16)
-        p_grouped = keep.tile([P, WORDS, GRID_ROWS, PACK], BF16, align_bytes=64)
+        p_grouped = keep.tile([P, PASSES, TOKENS, PACK], BF16, align_bytes=64)
         p_codes = keep.tile([P, PASSES, TOKENS], U32, align_bytes=64)
         p_scales = keep.tile([P, PASSES, TOKENS], U8, align_bytes=64)
         w1_grouped = keep.tile([P, HALVES, PASSES, F_HALF, PACK], BF16, align_bytes=64)
@@ -119,17 +118,23 @@ def tile_mlpconv2d_pa_s_kernel(tc, x, w1, b1, w2, b2, out):
                 )
 
         def gather_p(copy, n):
-            for odd in range(2):
-                copy(
-                    out=p_grouped[:].rearrange("p (s odd) a t -> p odd s a t", odd=2)[:, odd, :, n * GRID : (n + 1) * GRID],
-                    in_=spread[n][:, :, 2 * odd : 2 * odd + 2 * WORDS].rearrange("p u (s t) -> p s u t", t=PACK),
-                )
+            for g in range(PASSES):
+                for odd in range(2):
+                    first = PACK * g + 2 * odd
+                    place = odd * HALF_TOKENS + n * HALF_TOKENS // 2
+                    copy(
+                        out=p_grouped[:, g, place : place + HALF_TOKENS // 2, :].rearrange(
+                            "p (u w) t -> p u (w t)", w=GRID // 2
+                        ),
+                        in_=spread[n][:, :, first : first + 2 * GRID],
+                    )
 
         def quantise_p():
-            for g in range(PASSES):
-                quantise(
-                    p_codes[:, g], p_scales[:, g], p_grouped[:, 2 * g : 2 * g + GRID].rearrange("p s a t -> p (s a t)")
-                )
+            quantise(
+                p_codes[:].rearrange("p g r -> p (g r)"),
+                p_scales[:].rearrange("p g r -> p (g r)"),
+                p_grouped[:].rearrange("p g r t -> p (g r t)"),
+            )
 
         def regroup_w1(copy, half, g, lo, hi):
             regroup(copy, w1_grouped[:, half, g, lo:hi, :], w1_raw[:, half, g, :, lo:hi])
@@ -173,8 +178,8 @@ def tile_mlpconv2d_pa_s_kernel(tc, x, w1, b1, w2, b2, out):
         def bias_relu(half, t):
             m = PACK * half + t
             nc.scalar.activation(
-                out=h_relu[:, half, t, :].rearrange("p (a v) -> p a v", v=GRID),
-                in_=h_sum(half, t).rearrange("p (v a) -> p a v", v=GRID),
+                out=h_relu[:, half, t, :].rearrange("p (q odd) -> p q odd", odd=2),
+                in_=h_sum(half, t).rearrange("p (odd q) -> p q odd", odd=2),
                 func=RELU,
                 bias=bias_cols[:, m : m + 1],
             )

import concourse.mybir as mybir
from concourse.masks import make_identity

BF16 = mybir.dt.bfloat16
F32 = mybir.dt.float32
U32 = mybir.dt.uint32
U8 = mybir.dt.uint8
FP8X4 = mybir.dt.float8_e4m3fn_x4
ADD = mybir.AluOpType.add
RELU = mybir.ActivationFunctionType.Relu

P = 128
PACK = 4
PASSES = 2

IMAGES, CHANNELS, HEIGHT, WIDTH = 2, 16, 22, 22
WINDOW, STRIDE, GRID = 8, 2, 8
TOKENS = IMAGES * GRID * GRID
HALF_TOKENS = TOKENS // 2
F1 = 1024
F2 = 128
F_TILE = 128
F_HALF = PACK * F_TILE
HALVES = F1 // F_HALF
ROW_PAIRS = WINDOW // STRIDE
ROWS_KEPT = STRIDE * GRID
B1_ROWS = F1 // P
VECTOR_COLS = 256
LAST_V = 448

FLOPS = 2 * TOKENS * 1024 * F1 + 2 * TOKENS * F1 * F2


def regroup(copy, grouped, raw):
    copy(
        out=grouped.rearrange("p (c i) t -> p c t i", i=4),
        in_=raw.rearrange("p t (c i) -> p c t i", i=4),
    )


def tile_mlpconv2d_pa_s_kernel(tc, x, w1, b1, w2, b2, out):
    nc = tc.nc
    with tc.tile_pool(name="keep", bufs=1) as keep, tc.psum_pool(name="psum", bufs=1) as psum, tc.manual_schedule():

        def quantise(codes, scales, grouped):
            nc.vector.quantize_mx(out=codes.bitcast(FP8X4), scales=scales, in_=grouped)

        x_rows = keep.tile([P, ROWS_KEPT * WIDTH], BF16)
        select = keep.tile([P, IMAGES, STRIDE, P], BF16)
        bias_rows = keep.tile([P, P], BF16)
        warm = keep.tile([P, 2], F32)
        w1_raw = keep.tile([P, HALVES, PASSES, PACK, F_HALF], BF16)
        w2_raw = keep.tile([P, PASSES, PACK, F2], BF16)
        p_grouped = keep.tile([P, PASSES, TOKENS, PACK], BF16, align_bytes=64)
        p_codes = keep.tile([P, PASSES, TOKENS], U32, align_bytes=64)
        p_scales = keep.tile([P, PASSES, TOKENS], U8, align_bytes=64)
        w1_grouped = keep.tile([P, HALVES, PASSES, F_HALF, PACK], BF16, align_bytes=64)
        w1_codes = keep.tile([P, PASSES, F1], U32, align_bytes=64)
        w1_scales = keep.tile([P, PASSES, F1], U8, align_bytes=64)
        ident = keep.tile([P, P], BF16)
        spread = [psum.tile([P, GRID, WIDTH], BF16, name="spread_%d" % n, tag=tag) for n, tag in enumerate(("biases", "out"))]
        bias_cols = keep.tile([P, B1_ROWS + 1], BF16)
        b2_all = keep.tile([P, F2], F32)
        h_acc0 = psum.tile([P, PACK, TOKENS], F32)
        h_acc1 = [psum.tile([P, TOKENS], F32, name="h_acc1_%d" % t) for t in range(PACK)]
        h_relu = keep.tile([P, HALVES, PACK, TOKENS], BF16)
        h_grouped = keep.tile([P, HALVES, TOKENS, PACK], BF16, align_bytes=64)
        h_codes = keep.tile([P, HALVES, TOKENS], U32, align_bytes=64)
        h_scales = keep.tile([P, HALVES, TOKENS], U8, align_bytes=64)
        w2_grouped = keep.tile([P, PASSES, F2, PACK], BF16, align_bytes=64)
        w2_codes = keep.tile([P, PASSES, F2], U32, align_bytes=64)
        w2_scales = keep.tile([P, PASSES, F2], U8, align_bytes=64)
        idle_sums = psum.tile([P, 2 * F_TILE], F32)
        biased = keep.tile([P, F2], F32)
        result = keep.tile([P, F2], F32)

        def load_x(queue, a):
            queue.dma_start(
                out=x_rows[2 * CHANNELS * a : 2 * CHANNELS * (a + 1), :],
                in_=x[:, :, STRIDE * a : STRIDE * a + ROWS_KEPT, :].rearrange("n c h w -> (n c) (h w)"),
            )

        w1_view = w1.rearrange("(p g t) f -> p g t f", g=PASSES, t=PACK)

        def load_w1(half, g):
            nc.sync.dma_start(out=w1_raw[:, half, g], in_=w1_view[:, g, :, half * F_HALF : (half + 1) * F_HALF])

        nc.gpsimd.memset(warm[:, 0:1], 0.0)
        nc.gpsimd.memset(bias_rows[:], 0.0)
        for a in range(ROW_PAIRS):
            load_x(nc.scalar, a)
        load_w1(0, 0)
        nc.sync.dma_start(out=bias_rows[0:B1_ROWS, :], in_=b1.rearrange("(m p) -> m p", p=P))
        nc.sync.dma_start(out=bias_rows[B1_ROWS : B1_ROWS + 1, :], in_=b2.unsqueeze(0))
        load_w1(0, 1)
        load_w1(1, 0)
        load_w1(1, 1)
        nc.sync.dma_start(out=w2_raw[:], in_=w2.rearrange("(g t p) n -> p g t n", t=PACK, p=P))
        make_identity(nc, ident[:])
        nc.scalar.copy(out=warm[:, 1:2], in_=warm[:, 0:1])
        nc.vector.memset(select[:], 0.0)
        for n in range(IMAGES):
            for b in range(STRIDE):
                nc.vector.tensor_copy(
                    out=select[:, n, b].rearrange("p (c a b) -> p b c a", a=ROW_PAIRS, b=STRIDE)[:, b],
                    in_=ident[:].rearrange("p (a n c) -> p n c a", a=ROW_PAIRS, n=IMAGES)[:, n],
                )

        def spread_x(n):
            by_parity = x_rows[:].rearrange("p (u b w) -> p b u w", b=STRIDE, w=WIDTH)
            for b in range(STRIDE):
                nc.tensor.matmul(
                    out=spread[n][:],
                    lhsT=select[:, n, b],
                    rhs=by_parity[:, b],
                    start=(b == 0),
                    stop=(b == STRIDE - 1),
                )

        def gather_p(copy, n):
            for g in range(PASSES):
                for odd in range(2):
                    first = PACK * g + 2 * odd
                    place = odd * HALF_TOKENS + n * HALF_TOKENS // 2
                    copy(
                        out=p_grouped[:, g, place : place + HALF_TOKENS // 2, :].rearrange(
                            "p (u w) t -> p u (w t)", w=GRID // 2
                        ),
                        in_=spread[n][:, :, first : first + 2 * GRID],
                    )

        def quantise_p():
            quantise(
                p_codes[:].rearrange("p g r -> p (g r)"),
                p_scales[:].rearrange("p g r -> p (g r)"),
                p_grouped[:].rearrange("p g r t -> p (g r t)"),
            )

        def regroup_w1(copy, half, g, lo, hi):
            regroup(copy, w1_grouped[:, half, g, lo:hi, :], w1_raw[:, half, g, :, lo:hi])

        def quantise_w1(half, g, lo, hi):
            cols = slice(half * F_HALF + lo, half * F_HALF + hi)
            quantise(
                w1_codes[:, g, cols],
                w1_scales[:, g, cols],
                w1_grouped[:, half, g, lo:hi, :].rearrange("p f t -> p (f t)"),
            )

        def h_sum(half, t):
            return h_acc0[:, t, :] if half == 0 else h_acc1[t][:]

        def keep_clock_up(half, g, passes):
            cols = slice(half * F_HALF, half * F_HALF + 2 * F_TILE)
            for again in range(passes):
                nc.tensor.matmul_mx(
                    out=idle_sums[:],
                    lhsT=w1_codes[:, g, half * F_HALF : half * F_HALF + F_TILE].bitcast(FP8X4),
                    lhsT_scale=w1_scales[:, g, half * F_HALF : half * F_HALF + F_TILE],
                    rhs=w1_codes[:, g, cols].bitcast(FP8X4),
                    rhs_scale=w1_scales[:, g, cols],
                    start=True,
                    stop=True,
                )

        def first_layer(half, t, g):
            cols = slice(half * F_HALF + t * F_TILE, half * F_HALF + (t + 1) * F_TILE)
            nc.tensor.matmul_mx(
                out=h_sum(half, t),
                lhsT=w1_codes[:, g, cols].bitcast(FP8X4),
                lhsT_scale=w1_scales[:, g, cols],
                rhs=p_codes[:, g, :].bitcast(FP8X4),
                rhs_scale=p_scales[:, g, :],
                start=(g == 0),
                stop=(g == PASSES - 1),
            )

        def bias_relu(half, t):
            m = PACK * half + t
            nc.scalar.activation(
                out=h_relu[:, half, t, :].rearrange("p (q odd) -> p q odd", odd=2),
                in_=h_sum(half, t).rearrange("p (odd q) -> p q odd", odd=2),
                func=RELU,
                bias=bias_cols[:, m : m + 1],
            )

        def group_h(half, lo=0, hi=TOKENS):
            regroup(vcopy, h_grouped[:, half, lo:hi], h_relu[:, half, :, lo:hi])

        def quantise_h(half, lo=0, hi=TOKENS):
            quantise(
                h_codes[:, half, lo:hi], h_scales[:, half, lo:hi], h_grouped[:, half, lo:hi].rearrange("p r t -> p (r t)")
            )

        def quantise_w2():
            quantise(
                w2_codes[:].rearrange("p g n -> p (g n)"),
                w2_scales[:].rearrange("p g n -> p (g n)"),
                w2_grouped[:].rearrange("p g n t -> p (g n t)"),
            )

        def second_layer(half):
            nc.tensor.matmul_mx(
                out=out_acc[:],
                lhsT=h_codes[:, half, :].bitcast(FP8X4),
                lhsT_scale=h_scales[:, half, :],
                rhs=w2_codes[:, half, :].bitcast(FP8X4),
                rhs_scale=w2_scales[:, half, :],
                start=(half == 0),
                stop=(half == HALVES - 1),
            )

        V = VECTOR_COLS
        vcopy = nc.vector.tensor_copy
        scopy = nc.scalar.copy

        for n in range(IMAGES):
            spread_x(n)
        regroup_w1(vcopy, 0, 0, 0, V)
        regroup_w1(scopy, 0, 0, V, F_HALF)
        gather_p(vcopy, 0)
        gather_p(scopy, 1)
        quantise_w1(0, 0, 0, V)
        bias_turned = psum.tile([P, P], BF16, tag="biases")
        nc.tensor.transpose(out=bias_turned[:], in_=bias_rows[:], identity=ident[:])
        regroup_w1(vcopy, 0, 1, 0, V)
        regroup_w1(scopy, 0, 1, V, F_HALF)
        quantise_p()
        nc.scalar.copy(out=bias_cols[:], in_=bias_turned[:, 0 : B1_ROWS + 1])
        keep_clock_up(0, 0, 4)
        quantise_w1(0, 0, V, F_HALF)
        quantise_w1(0, 1, 0, V)
        regroup_w1(vcopy, 1, 0, 0, V)
        regroup_w1(scopy, 1, 0, V, F_HALF)
        quantise_w1(0, 1, V, F_HALF)
        for t in range(PACK):
            for g in range(PASSES):
                first_layer(0, t, g)
        keep_clock_up(0, 1, 1)
        quantise_w1(1, 0, 0, V)
        first_layer(1, 0, 0)
        first_layer(1, 1, 0)
        keep_clock_up(1, 0, 2)
        regroup_w1(vcopy, 1, 1, 0, V)
        regroup_w1(scopy, 1, 1, V, LAST_V)
        quantise_w1(1, 0, V, F_HALF)
        first_layer(1, 2, 0)
        first_layer(1, 3, 0)
        keep_clock_up(1, 0, 1)
        regroup_w1(vcopy, 1, 1, LAST_V, F_HALF)
        quantise_w1(1, 1, 0, V)
        first_layer(1, 0, 1)
        first_layer(1, 1, 1)
        for t in (2, 3):
            quantise_w1(1, 1, t * F_TILE, (t + 1) * F_TILE)
            first_layer(1, t, 1)
        for t in (3, 0, 1, 2):
            bias_relu(0, t)
        regroup(scopy, w2_grouped[:, 0], w2_raw[:, 0])
        regroup(vcopy, w2_grouped[:, 1], w2_raw[:, 1])
        group_h(0)
        quantise_w2()
        quantise_h(0)
        for t in range(PACK):
            bias_relu(1, t)
        b2_spread = psum.tile([P, F2], F32, tag="biases")
        nc.tensor.matmul(
            out=b2_spread[:],
            lhsT=bias_cols[:, B1_ROWS : B1_ROWS + 1].to_broadcast([P, P]),
            rhs=ident[:],
            start=True,
            stop=True,
        )
        out_acc = psum.tile([P, F2], F32, tag="out")
        second_layer(0)
        keep_clock_up(1, 1, 2)
        nc.scalar.copy(out=b2_all[:], in_=b2_spread[:])
        for step in (group_h, quantise_h):
            for lo in (0, TOKENS // 2):
                step(1, lo, lo + TOKENS // 2)
        second_layer(1)

        for step in range(2):
            for lo in (0, F2 // 2):
                cols = slice(lo, lo + F2 // 2)
                if step == 0:
                    nc.vector.tensor_tensor(out=biased[:, cols], in0=out_acc[:, cols], in1=b2_all[:, cols], op=ADD)
                else:
                    nc.vector.tensor_scalar_max(out=result[:, cols], in0=biased[:, cols], scalar1=0.0)
        nc.sync.dma_start(out=out.flatten_outer_dims(), in_=result[:])
